import numpy as np
import ml_dtypes


def mxq(x, axis, fmt="e4m3"):
    dtype, down = {"e4m3": (ml_dtypes.float8_e4m3fn, 7), "e5m2": (ml_dtypes.float8_e5m2, 14)}[fmt]
    v = np.moveaxis(np.asarray(x, np.float32).astype(ml_dtypes.bfloat16).astype(np.float64), axis, -1)
    blocks = v.reshape(v.shape[:-1] + (-1, 32))
    amax = np.abs(blocks).max(-1, keepdims=True)
    byte = np.maximum(np.where(amax > 0, np.frexp(amax)[1] - 1 + 127, 0) - down, 1)
    scale = np.exp2(byte - 127.0)
    codes = (blocks / scale).astype(np.float32).astype(dtype).astype(np.float64)
    return np.moveaxis((codes * scale).reshape(v.shape), -1, axis)


WIDE = False


def mx_kscale(k):
    if not WIDE:
        return np.ones(k)
    levels = np.array([10, -10, 5, -5, 0])
    a = np.random.permutation(np.resize(levels, k // 512 * 4)).reshape(k // 512, 4)
    idx = np.arange(k)
    return np.exp2(a[idx // 512, idx % 128 // 32])


BF16 = ml_dtypes.bfloat16


def bf(x):
    return np.asarray(x, np.float32).astype(BF16)


def f64(x):
    return np.asarray(x).astype(np.float64)


B, N, D, Q, HG, OG, HF, OF = 4, 32, 256, 512, 512, 512, 512, 256
K0 = 2 * D + Q
P = N * N


def setup_inputs():
    s = mx_kscale(K0)
    sx, sq = s[:D], s[2 * D:]
    sw = np.concatenate([sx, sx, sq])
    return {"x": bf(np.random.standard_normal((B, N, D)) * sx),
            "q": bf(np.random.standard_normal((B, Q)) * sq),
            "g_w0": bf(np.random.standard_normal((K0, HG)) / np.sqrt(K0) / sw[:, None]),
            "g_b0": bf(np.random.standard_normal(HG) * 0.3)}


def reference(x, q, g_w0, g_b0):
    x, q = f64(x), f64(q)
    xi = np.tile(x, (1, N, 1))
    xj = np.repeat(x, N, axis=1)
    qr = np.broadcast_to(q[:, None, :], (B, P, Q))
    pair = np.concatenate([xi, xj, qr], axis=2)
    return np.maximum((mxq(pair, 2, "e4m3") @ mxq(f64(g_w0), 0, "e4m3")) + f64(g_b0), 0.0)

@@ -1,0 +1,205 @@
+from contextlib import ExitStack
+
+import concourse.mybir as mybir
+from concourse.masks import make_identity
+
+FP8X4 = mybir.dt.float8_e4m3fn_x4
+BF16 = mybir.dt.bfloat16
+F32 = mybir.dt.float32
+I32 = mybir.dt.int32
+U32 = mybir.dt.uint32
+U8 = mybir.dt.uint8
+ADD = mybir.AluOpType.add
+RELU = mybir.ActivationFunctionType.Relu
+
+P = 128
+PACK = 4
+K_PASS = P * PACK
+
+B, N, D, Q, H = 4, 32, 256, 512, 512
+WORDS = D // 2
+
+RUN = 2
+ROWS = P // B
+I_STEPS = N // RUN
+GROUPS = N // RUN
+
+VECTOR_COLS = 256
+
+FLOPS = 2 * B * N * N * (2 * D + Q) * H
+
+
+def tile_relationnetwork_pa_kernel(tc, x, q, g_w0, g_b0, out):
+    nc = tc.nc
+    with ExitStack() as ctx:
+        keep = ctx.enter_context(tc.tile_pool(name="keep", bufs=1))
+        results = ctx.enter_context(tc.tile_pool(name="results", bufs=6))
+        psum_once = ctx.enter_context(tc.psum_pool(name="psum_once", bufs=1))
+        psum_steady = ctx.enter_context(tc.psum_pool(name="psum_steady", bufs=2))
+        psum_group = ctx.enter_context(tc.psum_pool(name="psum_group", bufs=4))
+
+        x_padded = keep.tile([P, 3 * D], BF16)
+        nc.vector.memset(x_padded[:, 0:D], 0.0)
+        nc.vector.memset(x_padded[:, 2 * D : 3 * D], 0.0)
+        nc.sync.dma_start(out=x_padded[:, D : 2 * D], in_=x.rearrange("b n d -> (b n) d"))
+
+        w_raw = []
+        for c in range(2):
+            raw = keep.tile([P, PACK, H], BF16, name="w_raw%d" % c)
+            rows = g_w0[c * K_PASS : (c + 1) * K_PASS, :]
+            nc.sync.dma_start(out=raw[:], in_=rows.rearrange("(p t) f -> p t f", t=PACK))
+            w_raw.append(raw)
+
+        q_cols = keep.tile([P, B, PACK], BF16)
+        with nc.allow_non_contiguous_dma(reason="512 pieces of four features of q"):
+            nc.scalar.dma_start(out=q_cols[:], in_=q.rearrange("b (p t) -> p b t", t=PACK))
+
+        bias_row = keep.tile([P, H], BF16)
+        nc.vector.memset(bias_row[:], 0.0)
+        nc.scalar.dma_start(out=bias_row[0:1, :], in_=g_b0.rearrange("(o f) -> o f", o=1))
+        ones = keep.tile([P, P], BF16)
+        nc.vector.memset(ones[:], 1.0)
+        identity = keep.tile([P, P], F32)
+        make_identity(nc, identity[:])
+
+        grouped_q = keep.tile([P, ROWS, B * PACK], BF16, align_bytes=64)
+        nc.vector.tensor_copy(
+            out=grouped_q[:],
+            in_=q_cols[:].rearrange("p b t -> p (b t)").unsqueeze(1).to_broadcast([P, ROWS, B * PACK]),
+        )
+        q_codes = keep.tile([P, P], U32, align_bytes=64)
+        q_scales = keep.tile([P, P], U8, align_bytes=64)
+        nc.vector.quantize_mx(
+            out=q_codes[:].bitcast(FP8X4),
+            scales=q_scales[:],
+            in_=grouped_q[:].rearrange("p r e -> p (r e)"),
+        )
+
+        x_words = x_padded[:].bitcast(F32)
+        x_t = psum_once.tile([P, 2, 2, P], F32)
+        for role in range(2):
+            first = (1 - role) * WORDS
+            for u in range(2):
+                nc.tensor.transpose(
+                    x_t[:, role, u, :], x_words[:, first + u : first + 2 * P : 2], identity[:]
+                )
+        grouped_x = keep.tile([P, 2 * N * B * PACK], BF16, align_bytes=64)
+        grouped_x_words = grouped_x[:].bitcast(F32).rearrange(
+            "p (o n b u) -> p o n b u", o=2, n=N, b=B
+        )
+        for role in range(2):
+            nc.scalar.copy(
+                out=grouped_x_words[:, role],
+                in_=x_t[:, role].rearrange("p u (b n) -> p n b u", b=B),
+            )
+        x_codes = keep.tile([P, 2 * P], U32, align_bytes=64)
+        x_scales = keep.tile([P, 2 * P], U8, align_bytes=64)
+        nc.vector.quantize_mx(
+            out=x_codes[:].bitcast(FP8X4), scales=x_scales[:], in_=grouped_x[:]
+        )
+        x_code_words = x_codes[:].bitcast(I32)
+        x_scale_words = x_scales[:].bitcast(I32)
+
+        w_codes = keep.tile([P, 2, H], U32, align_bytes=64)
+        w_scales = keep.tile([P, 2, H], U8, align_bytes=64)
+        cut = VECTOR_COLS // 4
+        for c in range(2):
+            grouped_w = keep.tile([P, H, PACK], BF16, name="grouped_w%d" % c, align_bytes=64)
+            dst = grouped_w[:].rearrange("p (c i) t -> p c t i", i=4)
+            src = w_raw[c][:].rearrange("p t (c i) -> p c t i", i=4)
+            nc.vector.tensor_copy(out=dst[:, :cut], in_=src[:, :cut])
+            nc.scalar.copy(out=dst[:, cut:], in_=src[:, cut:])
+            nc.vector.quantize_mx(
+                out=w_codes[:, c, :].bitcast(FP8X4),
+                scales=w_scales[:, c, :],
+                in_=grouped_w[:].rearrange("p f t -> p (f t)"),
+            )
+
+        xi_codes = keep.tile([P, RUN * P], U32, align_bytes=64)
+        xi_scales = keep.tile([P, RUN * P], U8, align_bytes=64)
+        xi_code_words = xi_codes[:].bitcast(I32).rearrange(
+            "p (s j i b) -> p s j i b", s=RUN, j=RUN, b=B
+        )
+        xi_scale_words = xi_scales[:].bitcast(I32).rearrange("p (s j i) -> p s j i", s=RUN, j=RUN)
+        for s in range(RUN):
+            nc.vector.tensor_copy(
+                out=xi_code_words[:, s],
+                in_=x_code_words[:, 0:P]
+                .rearrange("p (i s b) -> p s i b", s=RUN, b=B)[:, s]
+                .unsqueeze(1)
+                .to_broadcast([P, RUN, I_STEPS, B]),
+            )
+            nc.vector.tensor_copy(
+                out=xi_scale_words[:, s],
+                in_=x_scale_words[:, 0:N]
+                .rearrange("p (i s) -> p s i", s=RUN)[:, s]
+                .unsqueeze(1)
+                .to_broadcast([P, RUN, I_STEPS]),
+            )
+        xj_codes = keep.tile([P, GROUPS * P], U32, align_bytes=64)
+        xj_scales = keep.tile([P, GROUPS * P], U8, align_bytes=64)
+        nc.vector.tensor_copy(
+            out=xj_codes[:].bitcast(I32).rearrange("p (n i b) -> p n i b", n=N, b=B),
+            in_=x_code_words[:, P : 2 * P]
+            .rearrange("p (n b) -> p n b", b=B)
+            .unsqueeze(2)
+            .to_broadcast([P, N, I_STEPS, B]),
+        )
+        nc.vector.tensor_copy(
+            out=xj_scales[:].bitcast(I32).rearrange("p (n i) -> p n i", n=N),
+            in_=x_scale_words[:, N : 2 * N].unsqueeze(2).to_broadcast([P, N, I_STEPS]),
+        )
+
+        bias_ps = psum_once.tile([P, H], F32)
+        nc.tensor.matmul(out=bias_ps[:], lhsT=ones[:], rhs=bias_row[:], start=True, stop=True)
+        bias_all = keep.tile([P, H], F32)
+        nc.scalar.copy(out=bias_all[:], in_=bias_ps[:])
+        steady = keep.tile([P, RUN, H], F32)
+        for s in range(RUN):
+            cols = slice(s * P, (s + 1) * P)
+            steady_ps = psum_steady.tile([P, H], F32)
+            nc.tensor.matmul_mx(
+                out=steady_ps[:],
+                lhsT=xi_codes[:, cols].bitcast(FP8X4),
+                lhsT_scale=xi_scales[:, cols],
+                rhs=w_codes[:, 0, :].bitcast(FP8X4),
+                rhs_scale=w_scales[:, 0, :],
+                start=True,
+                stop=False,
+            )
+            nc.tensor.matmul_mx(
+                out=steady_ps[:],
+                lhsT=q_codes[:].bitcast(FP8X4),
+                lhsT_scale=q_scales[:],
+                rhs=w_codes[:, 1, :].bitcast(FP8X4),
+                rhs_scale=w_scales[:, 1, :],
+                start=False,
+                stop=True,
+            )
+            nc.vector.tensor_tensor(out=steady[:, s, :], in0=steady_ps[:], in1=bias_all[:], op=ADD)
+
+        out_runs = out.rearrange("b (g r s) f -> b g r (s f)", r=ROWS, s=RUN)
+        for g in range(GROUPS):
+            cols = slice(g * P, (g + 1) * P)
+            group_ps = psum_group.tile([P, H], F32)
+            nc.tensor.matmul_mx(
+                out=group_ps[:],
+                lhsT=xj_codes[:, cols].bitcast(FP8X4),
+                lhsT_scale=xj_scales[:, cols],
+                rhs=w_codes[:, 0, :].bitcast(FP8X4),
+                rhs_scale=w_scales[:, 0, :],
+                start=True,
+                stop=True,
+            )
+            result = results.tile([P, RUN, H], F32)
+            nc.vector.tensor_tensor(
+                out=result[:],
+                in0=group_ps[:].unsqueeze(1).to_broadcast([P, RUN, H]),
+                in1=steady[:],
+                op=ADD,
+            )
+            nc.scalar.activation(out=result[:], in_=result[:], func=RELU)
+            for b in range(B):
+                nc.sync.dma_start(
+                    out=out_runs[b, g], in_=result[b:P:B].rearrange("p s f -> p (s f)")
+                )

@@ -24,6 +24,9 @@ ROWS = P // B
 I_STEPS = N // RUN
 GROUPS = N // RUN
 
+AHEAD = 4
+SHARE = 4
+
 VECTOR_COLS = 256
 
 FLOPS = 2 * B * N * N * (2 * D + Q) * H
@@ -33,7 +36,9 @@ def tile_relationnetwork_pa_kernel(tc, x, q, g_w0, g_b0, out):
     nc = tc.nc
     with ExitStack() as ctx:
         keep = ctx.enter_context(tc.tile_pool(name="keep", bufs=1))
-        results = ctx.enter_context(tc.tile_pool(name="results", bufs=6))
+        operands = ctx.enter_context(tc.tile_pool(name="operands", bufs=GROUPS // AHEAD))
+        copies = ctx.enter_context(tc.tile_pool(name="copies", bufs=2))
+        results = ctx.enter_context(tc.tile_pool(name="results", bufs=8))
         psum_once = ctx.enter_context(tc.psum_pool(name="psum_once", bufs=1))
         psum_steady = ctx.enter_context(tc.psum_pool(name="psum_steady", bufs=2))
         psum_group = ctx.enter_context(tc.psum_pool(name="psum_group", bufs=4))
@@ -136,19 +141,27 @@ def tile_relationnetwork_pa_kernel(tc, x, q, g_w0, g_b0, out):
                 .unsqueeze(1)
                 .to_broadcast([P, RUN, I_STEPS]),
             )
-        xj_codes = keep.tile([P, GROUPS * P], U32, align_bytes=64)
-        xj_scales = keep.tile([P, GROUPS * P], U8, align_bytes=64)
-        nc.vector.tensor_copy(
-            out=xj_codes[:].bitcast(I32).rearrange("p (n i b) -> p n i b", n=N, b=B),
-            in_=x_code_words[:, P : 2 * P]
-            .rearrange("p (n b) -> p n b", b=B)
-            .unsqueeze(2)
-            .to_broadcast([P, N, I_STEPS, B]),
-        )
-        nc.vector.tensor_copy(
-            out=xj_scales[:].bitcast(I32).rearrange("p (n i) -> p n i", n=N),
-            in_=x_scale_words[:, N : 2 * N].unsqueeze(2).to_broadcast([P, N, I_STEPS]),
-        )
+        def fact_j_operands(first_group):
+            facts = AHEAD * RUN
+            n0 = first_group * RUN
+            codes = operands.tile([P, AHEAD * P], U32, name="xj_codes", align_bytes=64)
+            scales = operands.tile([P, AHEAD * P], U8, name="xj_scales", align_bytes=64)
+            nc.vector.tensor_copy(
+                out=codes[:].bitcast(I32).rearrange("p (n i b) -> p n i b", n=facts, b=B),
+                in_=x_code_words[:, P + n0 * B : P + (n0 + facts) * B]
+                .rearrange("p (n b) -> p n b", b=B)
+                .unsqueeze(2)
+                .to_broadcast([P, facts, I_STEPS, B]),
+            )
+            nc.vector.tensor_copy(
+                out=scales[:].bitcast(I32).rearrange("p (n i) -> p n i", n=facts),
+                in_=x_scale_words[:, N + n0 : N + n0 + facts]
+                .unsqueeze(2)
+                .to_broadcast([P, facts, I_STEPS]),
+            )
+            return codes, scales
+
+        xj_batches = [fact_j_operands(0)]
 
         bias_ps = psum_once.tile([P, H], F32)
         nc.tensor.matmul(out=bias_ps[:], lhsT=ones[:], rhs=bias_row[:], start=True, stop=True)
@@ -180,7 +193,10 @@ def tile_relationnetwork_pa_kernel(tc, x, q, g_w0, g_b0, out):
 
         out_runs = out.rearrange("b (g r s) f -> b g r (s f)", r=ROWS, s=RUN)
         for g in range(GROUPS):
-            cols = slice(g * P, (g + 1) * P)
+            if g % AHEAD == 0 and g + AHEAD < GROUPS:
+                xj_batches.append(fact_j_operands(g + AHEAD))
+            xj_codes, xj_scales = xj_batches[g // AHEAD]
+            cols = slice((g % AHEAD) * P, (g % AHEAD + 1) * P)
             group_ps = psum_group.tile([P, H], F32)
             nc.tensor.matmul_mx(
                 out=group_ps[:],
@@ -192,13 +208,24 @@ def tile_relationnetwork_pa_kernel(tc, x, q, g_w0, g_b0, out):
                 stop=True,
             )
             result = results.tile([P, RUN, H], F32)
-            nc.vector.tensor_tensor(
-                out=result[:],
-                in0=group_ps[:].unsqueeze(1).to_broadcast([P, RUN, H]),
-                in1=steady[:],
-                op=ADD,
-            )
-            nc.scalar.activation(out=result[:], in_=result[:], func=RELU)
+            if g % SHARE == 1:
+                group_sb = copies.tile([P, H], F32)
+                nc.scalar.copy(out=group_sb[:], in_=group_ps[:])
+                nc.gpsimd.tensor_tensor(
+                    out=result[:],
+                    in0=group_sb[:].unsqueeze(1).to_broadcast([P, RUN, H]),
+                    in1=steady[:],
+                    op=ADD,
+                )
+                nc.vector.tensor_scalar_max(out=result[:], in0=result[:], scalar1=0.0)
+            else:
+                nc.vector.tensor_tensor(
+                    out=result[:],
+                    in0=group_ps[:].unsqueeze(1).to_broadcast([P, RUN, H]),
+                    in1=steady[:],
+                    op=ADD,
+                )
+                nc.scalar.activation(out=result[:], in_=result[:], func=RELU)
             for b in range(B):
                 nc.sync.dma_start(
                     out=out_runs[b, g], in_=result[b:P:B].rearrange("p s f -> p (s f)")

@@ -17,15 +17,11 @@ PACK = 4
 K_PASS = P * PACK
 
 B, N, D, Q, H = 4, 32, 256, 512, 512
-WORDS = D // 2
 
 RUN = 2
 ROWS = P // B
 I_STEPS = N // RUN
 GROUPS = N // RUN
-
-AHEAD = 4
-SHARE = 4
 
 VECTOR_COLS = 256
 
@@ -35,37 +31,55 @@ FLOPS = 2 * B * N * N * (2 * D + Q) * H
 def tile_relationnetwork_pa_kernel(tc, x, q, g_w0, g_b0, out):
     nc = tc.nc
     with ExitStack() as ctx:
+        ctx.enter_context(tc.manual_schedule())
         keep = ctx.enter_context(tc.tile_pool(name="keep", bufs=1))
-        operands = ctx.enter_context(tc.tile_pool(name="operands", bufs=GROUPS // AHEAD))
-        copies = ctx.enter_context(tc.tile_pool(name="copies", bufs=2))
-        results = ctx.enter_context(tc.tile_pool(name="results", bufs=8))
-        psum_once = ctx.enter_context(tc.psum_pool(name="psum_once", bufs=1))
-        psum_steady = ctx.enter_context(tc.psum_pool(name="psum_steady", bufs=2))
-        psum_group = ctx.enter_context(tc.psum_pool(name="psum_group", bufs=4))
+        results = ctx.enter_context(tc.tile_pool(name="results", bufs=6))
+        psum = ctx.enter_context(tc.psum_pool(name="psum", bufs=8))
 
-        x_padded = keep.tile([P, 3 * D], BF16)
-        nc.vector.memset(x_padded[:, 0:D], 0.0)
-        nc.vector.memset(x_padded[:, 2 * D : 3 * D], 0.0)
-        nc.sync.dma_start(out=x_padded[:, D : 2 * D], in_=x.rearrange("b n d -> (b n) d"))
-
+        x_twice = keep.tile([P, 2, D], BF16)
+        for side in range(2):
+            nc.sync.dma_start(out=x_twice[:, side, :], in_=x.rearrange("b n d -> (b n) d"))
+        q_cols = keep.tile([P, B, PACK], BF16)
+        with nc.allow_non_contiguous_dma(reason="512 pieces of four features of q"):
+            nc.sync.dma_start(out=q_cols[:], in_=q.rearrange("b (p t) -> p b t", t=PACK))
         w_raw = []
         for c in range(2):
             raw = keep.tile([P, PACK, H], BF16, name="w_raw%d" % c)
             rows = g_w0[c * K_PASS : (c + 1) * K_PASS, :]
             nc.sync.dma_start(out=raw[:], in_=rows.rearrange("(p t) f -> p t f", t=PACK))
             w_raw.append(raw)
-
-        q_cols = keep.tile([P, B, PACK], BF16)
-        with nc.allow_non_contiguous_dma(reason="512 pieces of four features of q"):
-            nc.scalar.dma_start(out=q_cols[:], in_=q.rearrange("b (p t) -> p b t", t=PACK))
-
         bias_row = keep.tile([P, H], BF16)
         nc.vector.memset(bias_row[:], 0.0)
-        nc.scalar.dma_start(out=bias_row[0:1, :], in_=g_b0.rearrange("(o f) -> o f", o=1))
+        nc.sync.dma_start(out=bias_row[0:1, :], in_=g_b0.rearrange("(o f) -> o f", o=1))
+
+        grouped_x = keep.tile([P, 2 * N * B * PACK], BF16, align_bytes=64)
+        nc.vector.memset(grouped_x[:], 0.0)
         ones = keep.tile([P, P], BF16)
         nc.vector.memset(ones[:], 1.0)
         identity = keep.tile([P, P], F32)
         make_identity(nc, identity[:])
+
+        w_grouped = []
+        for c in range(2):
+            w_grouped.append(
+                keep.tile([P, H, PACK], BF16, name="w_grouped%d" % c, align_bytes=64)
+            )
+        w_codes = keep.tile([P, 2, H], U32, align_bytes=64)
+        w_scales = keep.tile([P, 2, H], U8, align_bytes=64)
+        cut = VECTOR_COLS // 4
+
+        def regroup_w(c):
+            dst = w_grouped[c][:].rearrange("p (c i) t -> p c t i", i=4)
+            src = w_raw[c][:].rearrange("p t (c i) -> p c t i", i=4)
+            nc.vector.tensor_copy(out=dst[:, :cut], in_=src[:, :cut])
+            nc.scalar.copy(out=dst[:, cut:], in_=src[:, cut:])
+
+        def quantise_w(c):
+            nc.vector.quantize_mx(
+                out=w_codes[:, c, :].bitcast(FP8X4),
+                scales=w_scales[:, c, :],
+                in_=w_grouped[c][:].rearrange("p f t -> p (f t)"),
+            )
 
         grouped_q = keep.tile([P, ROWS, B * PACK], BF16, align_bytes=64)
         nc.vector.tensor_copy(
@@ -80,23 +94,22 @@ def tile_relationnetwork_pa_kernel(tc, x, q, g_w0, g_b0, out):
             in_=grouped_q[:].rearrange("p r e -> p (r e)"),
         )
 
-        x_words = x_padded[:].bitcast(F32)
-        x_t = psum_once.tile([P, 2, 2, P], F32)
-        for role in range(2):
-            first = (1 - role) * WORDS
-            for u in range(2):
-                nc.tensor.transpose(
-                    x_t[:, role, u, :], x_words[:, first + u : first + 2 * P : 2], identity[:]
-                )
-        grouped_x = keep.tile([P, 2 * N * B * PACK], BF16, align_bytes=64)
+        x_words = x_twice[:].rearrange("p c d -> p (c d)").bitcast(F32)
+        x_t = psum.tile([P, 2, P], F32, tag="bank")
+        for u in range(2):
+            nc.tensor.transpose(x_t[:, u, :], x_words[:, u : 2 * P : 2], identity[:])
         grouped_x_words = grouped_x[:].bitcast(F32).rearrange(
             "p (o n b u) -> p o n b u", o=2, n=N, b=B
         )
         for role in range(2):
+            half = slice(role * (P // 2), (role + 1) * (P // 2))
             nc.scalar.copy(
-                out=grouped_x_words[:, role],
-                in_=x_t[:, role].rearrange("p u (b n) -> p n b u", b=B),
+                out=grouped_x_words[half, role],
+                in_=x_t[half].rearrange("p u (b n) -> p n b u", b=B),
             )
+
+        regroup_w(0)
+
         x_codes = keep.tile([P, 2 * P], U32, align_bytes=64)
         x_scales = keep.tile([P, 2 * P], U8, align_bytes=64)
         nc.vector.quantize_mx(
@@ -104,21 +117,6 @@ def tile_relationnetwork_pa_kernel(tc, x, q, g_w0, g_b0, out):
         )
         x_code_words = x_codes[:].bitcast(I32)
         x_scale_words = x_scales[:].bitcast(I32)
-
-        w_codes = keep.tile([P, 2, H], U32, align_bytes=64)
-        w_scales = keep.tile([P, 2, H], U8, align_bytes=64)
-        cut = VECTOR_COLS // 4
-        for c in range(2):
-            grouped_w = keep.tile([P, H, PACK], BF16, name="grouped_w%d" % c, align_bytes=64)
-            dst = grouped_w[:].rearrange("p (c i) t -> p c t i", i=4)
-            src = w_raw[c][:].rearrange("p t (c i) -> p c t i", i=4)
-            nc.vector.tensor_copy(out=dst[:, :cut], in_=src[:, :cut])
-            nc.scalar.copy(out=dst[:, cut:], in_=src[:, cut:])
-            nc.vector.quantize_mx(
-                out=w_codes[:, c, :].bitcast(FP8X4),
-                scales=w_scales[:, c, :],
-                in_=grouped_w[:].rearrange("p f t -> p (f t)"),
-            )
 
         xi_codes = keep.tile([P, RUN * P], U32, align_bytes=64)
         xi_scales = keep.tile([P, RUN * P], U8, align_bytes=64)
@@ -141,36 +139,35 @@ def tile_relationnetwork_pa_kernel(tc, x, q, g_w0, g_b0, out):
                 .unsqueeze(1)
                 .to_broadcast([P, RUN, I_STEPS]),
             )
-        def fact_j_operands(first_group):
-            facts = AHEAD * RUN
-            n0 = first_group * RUN
-            codes = operands.tile([P, AHEAD * P], U32, name="xj_codes", align_bytes=64)
-            scales = operands.tile([P, AHEAD * P], U8, name="xj_scales", align_bytes=64)
-            nc.vector.tensor_copy(
-                out=codes[:].bitcast(I32).rearrange("p (n i b) -> p n i b", n=facts, b=B),
-                in_=x_code_words[:, P + n0 * B : P + (n0 + facts) * B]
-                .rearrange("p (n b) -> p n b", b=B)
-                .unsqueeze(2)
-                .to_broadcast([P, facts, I_STEPS, B]),
-            )
-            nc.vector.tensor_copy(
-                out=scales[:].bitcast(I32).rearrange("p (n i) -> p n i", n=facts),
-                in_=x_scale_words[:, N + n0 : N + n0 + facts]
-                .unsqueeze(2)
-                .to_broadcast([P, facts, I_STEPS]),
-            )
-            return codes, scales
 
-        xj_batches = [fact_j_operands(0)]
+        quantise_w(0)
 
-        bias_ps = psum_once.tile([P, H], F32)
+        regroup_w(1)
+        quantise_w(1)
+
+        xj_codes = keep.tile([P, GROUPS * P], U32, align_bytes=64)
+        xj_scales = keep.tile([P, GROUPS * P], U8, align_bytes=64)
+        nc.vector.tensor_copy(
+            out=xj_codes[:].bitcast(I32).rearrange("p (n i b) -> p n i b", n=N, b=B),
+            in_=x_code_words[:, P : 2 * P]
+            .rearrange("p (n b) -> p n b", b=B)
+            .unsqueeze(2)
+            .to_broadcast([P, N, I_STEPS, B]),
+        )
+        nc.vector.tensor_copy(
+            out=xj_scales[:].bitcast(I32).rearrange("p (n i) -> p n i", n=N),
+            in_=x_scale_words[:, N : 2 * N].unsqueeze(2).to_broadcast([P, N, I_STEPS]),
+        )
+
+        bias_ps = psum.tile([P, H], F32, tag="bank")
         nc.tensor.matmul(out=bias_ps[:], lhsT=ones[:], rhs=bias_row[:], start=True, stop=True)
         bias_all = keep.tile([P, H], F32)
         nc.scalar.copy(out=bias_all[:], in_=bias_ps[:])
         steady = keep.tile([P, RUN, H], F32)
+        steady_banks = []
         for s in range(RUN):
             cols = slice(s * P, (s + 1) * P)
-            steady_ps = psum_steady.tile([P, H], F32)
+            steady_ps = psum.tile([P, H], F32, name="steady_ps", tag="bank")
             nc.tensor.matmul_mx(
                 out=steady_ps[:],
                 lhsT=xi_codes[:, cols].bitcast(FP8X4),
@@ -180,8 +177,10 @@ def tile_relationnetwork_pa_kernel(tc, x, q, g_w0, g_b0, out):
                 start=True,
                 stop=False,
             )
+            steady_banks.append(steady_ps)
+        for s in range(RUN):
             nc.tensor.matmul_mx(
-                out=steady_ps[:],
+                out=steady_banks[s][:],
                 lhsT=q_codes[:].bitcast(FP8X4),
                 lhsT_scale=q_scales[:],
                 rhs=w_codes[:, 1, :].bitcast(FP8X4),
@@ -189,15 +188,14 @@ def tile_relationnetwork_pa_kernel(tc, x, q, g_w0, g_b0, out):
                 start=False,
                 stop=True,
             )
-            nc.vector.tensor_tensor(out=steady[:, s, :], in0=steady_ps[:], in1=bias_all[:], op=ADD)
+            nc.vector.tensor_tensor(
+                out=steady[:, s, :], in0=steady_banks[s][:], in1=bias_all[:], op=ADD
+            )
 
         out_runs = out.rearrange("b (g r s) f -> b g r (s f)", r=ROWS, s=RUN)
         for g in range(GROUPS):
-            if g % AHEAD == 0 and g + AHEAD < GROUPS:
-                xj_batches.append(fact_j_operands(g + AHEAD))
-            xj_codes, xj_scales = xj_batches[g // AHEAD]
-            cols = slice((g % AHEAD) * P, (g % AHEAD + 1) * P)
-            group_ps = psum_group.tile([P, H], F32)
+            cols = slice(g * P, (g + 1) * P)
+            group_ps = psum.tile([P, H], F32, tag="bank")
             nc.tensor.matmul_mx(
                 out=group_ps[:],
                 lhsT=xj_codes[:, cols].bitcast(FP8X4),
@@ -208,24 +206,16 @@ def tile_relationnetwork_pa_kernel(tc, x, q, g_w0, g_b0, out):
                 stop=True,
             )
             result = results.tile([P, RUN, H], F32)
-            if g % SHARE == 1:
-                group_sb = copies.tile([P, H], F32)
-                nc.scalar.copy(out=group_sb[:], in_=group_ps[:])
-                nc.gpsimd.tensor_tensor(
-                    out=result[:],
-                    in0=group_sb[:].unsqueeze(1).to_broadcast([P, RUN, H]),
-                    in1=steady[:],
-                    op=ADD,
-                )
-                nc.vector.tensor_scalar_max(out=result[:], in0=result[:], scalar1=0.0)
-            else:
-                nc.vector.tensor_tensor(
-                    out=result[:],
-                    in0=group_ps[:].unsqueeze(1).to_broadcast([P, RUN, H]),
-                    in1=steady[:],
-                    op=ADD,
-                )
+            nc.vector.tensor_tensor(
+                out=result[:],
+                in0=group_ps[:].unsqueeze(1).to_broadcast([P, RUN, H]),
+                in1=steady[:],
+                op=ADD,
+            )
+            if g < GROUPS - 1:
                 nc.scalar.activation(out=result[:], in_=result[:], func=RELU)
+            else:
+                nc.vector.tensor_scalar_max(out=result[:], in0=result[:], scalar1=0.0)
             for b in range(B):
                 nc.sync.dma_start(
                     out=out_runs[b, g], in_=result[b:P:B].rearrange("p s f -> p (s f)")

@@ -13,15 +13,15 @@ ADD = mybir.AluOpType.add
 RELU = mybir.ActivationFunctionType.Relu
 
 P = 128
+HALF = P // 2
 PACK = 4
 K_PASS = P * PACK
 
 B, N, D, Q, H = 4, 32, 256, 512, 512
-
+COPIES = 4
+BATCH = 4
 RUN = 2
-ROWS = P // B
-I_STEPS = N // RUN
-GROUPS = N // RUN
+EARLY_BATCHES = 2
 
 VECTOR_COLS = 256
 
@@ -33,31 +33,35 @@ def tile_relationnetwork_pa_kernel(tc, x, q, g_w0, g_b0, out):
     with ExitStack() as ctx:
         ctx.enter_context(tc.manual_schedule())
         keep = ctx.enter_context(tc.tile_pool(name="keep", bufs=1))
-        results = ctx.enter_context(tc.tile_pool(name="results", bufs=6))
+        operands = ctx.enter_context(tc.tile_pool(name="operands", bufs=EARLY_BATCHES))
+        results = ctx.enter_context(tc.tile_pool(name="results", bufs=8))
         psum = ctx.enter_context(tc.psum_pool(name="psum", bufs=8))
+
+        first = keep.tile([P, 1], F32)
+        nc.vector.memset(first[:], 0.0)
+        rows = keep.tile([P, 2, H], BF16)
+        nc.vector.memset(rows[:].rearrange("p a f -> p (a f)").bitcast(I32), 0)
+        ones = keep.tile([P, P], BF16)
+        nc.vector.memset(ones[:], 1.0)
+        grouped_xj = keep.tile([P, P * PACK], BF16, align_bytes=64)
+        nc.vector.memset(grouped_xj[0:HALF, :].bitcast(I32), 0)
+        grouped_xi = keep.tile([P, P * COPIES * PACK], BF16, align_bytes=64)
+        nc.vector.memset(grouped_xi[HALF:P, :].bitcast(I32), 0)
+        identity = keep.tile([P, P], F32)
+        make_identity(nc, identity[:])
+        nc.scalar.activation(out=first[:], in_=first[:], func=RELU)
 
         x_twice = keep.tile([P, 2, D], BF16)
         for side in range(2):
             nc.sync.dma_start(out=x_twice[:, side, :], in_=x.rearrange("b n d -> (b n) d"))
-        q_cols = keep.tile([P, B, PACK], BF16)
-        with nc.allow_non_contiguous_dma(reason="512 pieces of four features of q"):
-            nc.sync.dma_start(out=q_cols[:], in_=q.rearrange("b (p t) -> p b t", t=PACK))
+        nc.sync.dma_start(out=rows[0:B, 0, :], in_=q)
         w_raw = []
         for c in range(2):
             raw = keep.tile([P, PACK, H], BF16, name="w_raw%d" % c)
-            rows = g_w0[c * K_PASS : (c + 1) * K_PASS, :]
-            nc.sync.dma_start(out=raw[:], in_=rows.rearrange("(p t) f -> p t f", t=PACK))
+            w_rows = g_w0[c * K_PASS : (c + 1) * K_PASS, :]
+            nc.sync.dma_start(out=raw[:], in_=w_rows.rearrange("(p t) f -> p t f", t=PACK))
             w_raw.append(raw)
-        bias_row = keep.tile([P, H], BF16)
-        nc.vector.memset(bias_row[:], 0.0)
-        nc.sync.dma_start(out=bias_row[0:1, :], in_=g_b0.rearrange("(o f) -> o f", o=1))
-
-        grouped_x = keep.tile([P, 2 * N * B * PACK], BF16, align_bytes=64)
-        nc.vector.memset(grouped_x[:], 0.0)
-        ones = keep.tile([P, P], BF16)
-        nc.vector.memset(ones[:], 1.0)
-        identity = keep.tile([P, P], F32)
-        make_identity(nc, identity[:])
+        nc.sync.dma_start(out=rows[0:1, 1, :], in_=g_b0.rearrange("(o f) -> o f", o=1))
 
         w_grouped = []
         for c in range(2):
@@ -81,142 +85,142 @@ def tile_relationnetwork_pa_kernel(tc, x, q, g_w0, g_b0, out):
                 in_=w_grouped[c][:].rearrange("p f t -> p (f t)"),
             )
 
-        grouped_q = keep.tile([P, ROWS, B * PACK], BF16, align_bytes=64)
-        nc.vector.tensor_copy(
-            out=grouped_q[:],
-            in_=q_cols[:].rearrange("p b t -> p (b t)").unsqueeze(1).to_broadcast([P, ROWS, B * PACK]),
-        )
-        q_codes = keep.tile([P, P], U32, align_bytes=64)
-        q_scales = keep.tile([P, P], U8, align_bytes=64)
-        nc.vector.quantize_mx(
-            out=q_codes[:].bitcast(FP8X4),
-            scales=q_scales[:],
-            in_=grouped_q[:].rearrange("p r e -> p (r e)"),
-        )
+        def product(bank, codes, scales, c, start, stop):
+            nc.tensor.matmul_mx(
+                out=bank[:],
+                lhsT=codes.bitcast(FP8X4),
+                lhsT_scale=scales,
+                rhs=w_codes[:, c, :].bitcast(FP8X4),
+                rhs_scale=w_scales[:, c, :],
+                start=start,
+                stop=stop,
+            )
 
         x_words = x_twice[:].rearrange("p c d -> p (c d)").bitcast(F32)
-        x_t = psum.tile([P, 2, P], F32, tag="bank")
+        x_t = []
+        for reader in range(2):
+            x_ps = psum.tile([P, 2, P], F32, name="x_ps", tag="bank")
+            for u in range(2):
+                nc.tensor.transpose(x_ps[:, u, :], x_words[:, u : 2 * P : 2], identity[:])
+            x_t.append(x_ps)
+        q_words = rows[:, 0, :].bitcast(F32)
+        q_ps = psum.tile([P, 2, P], F32, tag="bank")
         for u in range(2):
-            nc.tensor.transpose(x_t[:, u, :], x_words[:, u : 2 * P : 2], identity[:])
-        grouped_x_words = grouped_x[:].bitcast(F32).rearrange(
-            "p (o n b u) -> p o n b u", o=2, n=N, b=B
+            nc.tensor.transpose(q_ps[:, u, :], q_words[:, u : 2 * P : 2], identity[:])
+
+        xi_words = grouped_xi[0:HALF, :].bitcast(F32).rearrange(
+            "p (m r u) -> p m r u", r=COPIES, u=2
         )
-        for role in range(2):
-            half = slice(role * (P // 2), (role + 1) * (P // 2))
-            nc.scalar.copy(
-                out=grouped_x_words[half, role],
-                in_=x_t[half].rearrange("p u (b n) -> p n b u", b=B),
+        for reader, copy in enumerate((nc.scalar.copy, nc.vector.tensor_copy)):
+            facts = slice(reader * HALF, (reader + 1) * HALF)
+            copy(
+                out=xi_words[:, facts],
+                in_=x_t[reader][0:HALF, :, facts]
+                .rearrange("p u m -> p m u")
+                .unsqueeze(2)
+                .to_broadcast([HALF, HALF, COPIES, 2]),
             )
+        grouped_q = keep.tile([P, P * PACK], BF16, align_bytes=64)
+        nc.scalar.copy(
+            out=grouped_q[:].bitcast(F32).rearrange("p (b j u) -> p b j u", b=B, u=2),
+            in_=q_ps[:, :, 0:B]
+            .rearrange("p u b -> p b u")
+            .unsqueeze(2)
+            .to_broadcast([P, B, N, 2]),
+        )
+        nc.scalar.copy(
+            out=grouped_xj[HALF:P, :].bitcast(F32).rearrange("p (m u) -> p m u", u=2),
+            in_=x_t[0][HALF:P].rearrange("p u m -> p m u"),
+        )
+
+        def quantise(grouped, name):
+            columns = grouped.shape[1] // PACK
+            codes = keep.tile([P, columns], U32, name=name + "_codes", align_bytes=64)
+            scales = keep.tile([P, columns], U8, name=name + "_scales", align_bytes=64)
+            nc.vector.quantize_mx(
+                out=codes[:].bitcast(FP8X4), scales=scales[:], in_=grouped[:]
+            )
+            return codes, scales
+
+        xi_codes, xi_scales = quantise(grouped_xi, "xi")
+
+        step_scales = keep.tile([P, N, P], U8, align_bytes=64)
+        step_scale_words = step_scales[:].rearrange("p i m -> p (i m)").bitcast(I32).rearrange(
+            "p (i b w) -> p i b w", i=N, b=B
+        )
+        fact_scale_words = xi_scales[:].bitcast(I32).rearrange("p (b i) -> p i b", b=B)
+        fact_codes = xi_codes[:].bitcast(I32).rearrange("p (b i r) -> p i b r", b=B, r=COPIES)
+
+        def spread_scales(i0, i1):
+            nc.vector.tensor_copy(
+                out=step_scale_words[:, i0:i1],
+                in_=fact_scale_words[:, i0:i1]
+                .unsqueeze(3)
+                .to_broadcast([P, i1 - i0, B, N // COPIES]),
+            )
+
+        batches = {}
+
+        def spread_codes(batch, copy, at_once):
+            codes = operands.tile([P, BATCH * P], U32, name="step_codes", align_bytes=64)
+            words = codes[:].bitcast(I32).rearrange("p (i b j) -> p i b j", i=BATCH, b=B)
+            for k in range(0, BATCH, at_once):
+                i0 = batch * BATCH + k
+                copy(
+                    out=words[:, k : k + at_once],
+                    in_=fact_codes[:, i0 : i0 + at_once, :, 0]
+                    .unsqueeze(3)
+                    .to_broadcast([P, at_once, B, N]),
+                )
+            batches[batch] = codes
+
+        spread_codes(0, nc.vector.tensor_copy, BATCH)
+        spread_scales(0, EARLY_BATCHES * BATCH)
+        q_codes, q_scales = quantise(grouped_q, "q")
+        xj_codes, xj_scales = quantise(grouped_xj, "xj")
 
         regroup_w(0)
-
-        x_codes = keep.tile([P, 2 * P], U32, align_bytes=64)
-        x_scales = keep.tile([P, 2 * P], U8, align_bytes=64)
-        nc.vector.quantize_mx(
-            out=x_codes[:].bitcast(FP8X4), scales=x_scales[:], in_=grouped_x[:]
-        )
-        x_code_words = x_codes[:].bitcast(I32)
-        x_scale_words = x_scales[:].bitcast(I32)
-
-        xi_codes = keep.tile([P, RUN * P], U32, align_bytes=64)
-        xi_scales = keep.tile([P, RUN * P], U8, align_bytes=64)
-        xi_code_words = xi_codes[:].bitcast(I32).rearrange(
-            "p (s j i b) -> p s j i b", s=RUN, j=RUN, b=B
-        )
-        xi_scale_words = xi_scales[:].bitcast(I32).rearrange("p (s j i) -> p s j i", s=RUN, j=RUN)
-        for s in range(RUN):
-            nc.vector.tensor_copy(
-                out=xi_code_words[:, s],
-                in_=x_code_words[:, 0:P]
-                .rearrange("p (i s b) -> p s i b", s=RUN, b=B)[:, s]
-                .unsqueeze(1)
-                .to_broadcast([P, RUN, I_STEPS, B]),
-            )
-            nc.vector.tensor_copy(
-                out=xi_scale_words[:, s],
-                in_=x_scale_words[:, 0:N]
-                .rearrange("p (i s) -> p s i", s=RUN)[:, s]
-                .unsqueeze(1)
-                .to_broadcast([P, RUN, I_STEPS]),
-            )
-
         quantise_w(0)
-
         regroup_w(1)
         quantise_w(1)
 
-        xj_codes = keep.tile([P, GROUPS * P], U32, align_bytes=64)
-        xj_scales = keep.tile([P, GROUPS * P], U8, align_bytes=64)
-        nc.vector.tensor_copy(
-            out=xj_codes[:].bitcast(I32).rearrange("p (n i b) -> p n i b", n=N, b=B),
-            in_=x_code_words[:, P : 2 * P]
-            .rearrange("p (n b) -> p n b", b=B)
-            .unsqueeze(2)
-            .to_broadcast([P, N, I_STEPS, B]),
-        )
-        nc.vector.tensor_copy(
-            out=xj_scales[:].bitcast(I32).rearrange("p (n i) -> p n i", n=N),
-            in_=x_scale_words[:, N : 2 * N].unsqueeze(2).to_broadcast([P, N, I_STEPS]),
-        )
-
         bias_ps = psum.tile([P, H], F32, tag="bank")
-        nc.tensor.matmul(out=bias_ps[:], lhsT=ones[:], rhs=bias_row[:], start=True, stop=True)
+        nc.tensor.matmul(out=bias_ps[:], lhsT=ones[:], rhs=rows[:, 1, :], start=True, stop=True)
         bias_all = keep.tile([P, H], F32)
         nc.scalar.copy(out=bias_all[:], in_=bias_ps[:])
-        steady = keep.tile([P, RUN, H], F32)
-        steady_banks = []
-        for s in range(RUN):
-            cols = slice(s * P, (s + 1) * P)
-            steady_ps = psum.tile([P, H], F32, name="steady_ps", tag="bank")
-            nc.tensor.matmul_mx(
-                out=steady_ps[:],
-                lhsT=xi_codes[:, cols].bitcast(FP8X4),
-                lhsT_scale=xi_scales[:, cols],
-                rhs=w_codes[:, 0, :].bitcast(FP8X4),
-                rhs_scale=w_scales[:, 0, :],
-                start=True,
-                stop=False,
-            )
-            steady_banks.append(steady_ps)
-        for s in range(RUN):
-            nc.tensor.matmul_mx(
-                out=steady_banks[s][:],
-                lhsT=q_codes[:].bitcast(FP8X4),
-                lhsT_scale=q_scales[:],
-                rhs=w_codes[:, 1, :].bitcast(FP8X4),
-                rhs_scale=w_scales[:, 1, :],
-                start=False,
-                stop=True,
-            )
-            nc.vector.tensor_tensor(
-                out=steady[:, s, :], in0=steady_banks[s][:], in1=bias_all[:], op=ADD
-            )
+        steady_ps = psum.tile([P, H], F32, tag="bank")
+        product(steady_ps, xj_codes[:], xj_scales[:], 0, True, False)
+        product(steady_ps, q_codes[:], q_scales[:], 1, False, True)
+        steady = keep.tile([P, H], F32)
+        nc.vector.tensor_tensor(out=steady[:], in0=steady_ps[:], in1=bias_all[:], op=ADD)
+        spread_codes(1, nc.vector.tensor_copy, BATCH)
 
-        out_runs = out.rearrange("b (g r s) f -> b g r (s f)", r=ROWS, s=RUN)
-        for g in range(GROUPS):
-            cols = slice(g * P, (g + 1) * P)
-            group_ps = psum.tile([P, H], F32, tag="bank")
-            nc.tensor.matmul_mx(
-                out=group_ps[:],
-                lhsT=xj_codes[:, cols].bitcast(FP8X4),
-                lhsT_scale=xj_scales[:, cols],
-                rhs=w_codes[:, 0, :].bitcast(FP8X4),
-                rhs_scale=w_scales[:, 0, :],
-                start=True,
-                stop=True,
-            )
+        out_rows = out.rearrange("b (j i) f -> (b j) i f", i=N)
+        for i0 in range(0, N, RUN):
             result = results.tile([P, RUN, H], F32)
-            nc.vector.tensor_tensor(
-                out=result[:],
-                in0=group_ps[:].unsqueeze(1).to_broadcast([P, RUN, H]),
-                in1=steady[:],
-                op=ADD,
-            )
-            if g < GROUPS - 1:
-                nc.scalar.activation(out=result[:], in_=result[:], func=RELU)
-            else:
-                nc.vector.tensor_scalar_max(out=result[:], in0=result[:], scalar1=0.0)
-            for b in range(B):
-                nc.sync.dma_start(
-                    out=out_runs[b, g], in_=result[b:P:B].rearrange("p s f -> p (s f)")
+            apart = i0 == 0 or i0 == N - RUN
+            for s in range(RUN):
+                i = i0 + s
+                batch, k = divmod(i, BATCH)
+                bank = psum.tile([P, H], F32, name="step_ps", tag="bank")
+                product(
+                    bank, batches[batch][:, k * P : (k + 1) * P], step_scales[:, i, :], 0, True, True
                 )
+                nc.vector.tensor_tensor(
+                    out=result[:, s, :], in0=bank[:], in1=steady[:], op=ADD
+                )
+                if apart:
+                    if i < N - 1:
+                        nc.scalar.activation(out=result[:, s, :], in_=result[:, s, :], func=RELU)
+                    else:
+                        nc.vector.tensor_scalar_max(
+                            out=result[:, s, :], in0=result[:, s, :], scalar1=0.0
+                        )
+                    nc.sync.dma_start(out=out_rows[:, i, :], in_=result[:, s, :])
+                if i == 1:
+                    spread_scales(EARLY_BATCHES * BATCH, N)
+                if k == BATCH - 1 and batch + EARLY_BATCHES < N // BATCH:
+                    spread_codes(batch + EARLY_BATCHES, nc.gpsimd.tensor_copy, 2)
+            if not apart:
+                nc.scalar.activation(out=result[:], in_=result[:], func=RELU)
+                nc.sync.dma_start(out=out_rows[:, i0 : i0 + RUN, :], in_=result[:])

@@ -22,8 +22,10 @@ COPIES = 4
 BATCH = 4
 RUN = 2
 EARLY_BATCHES = 2
+WARM = (3, 2)
+EDGE = 4
 
-VECTOR_COLS = 256
+VECTOR_COLS = 208
 
 FLOPS = 2 * B * N * N * (2 * D + Q) * H
 
@@ -37,31 +39,36 @@ def tile_relationnetwork_pa_kernel(tc, x, q, g_w0, g_b0, out):
         results = ctx.enter_context(tc.tile_pool(name="results", bufs=8))
         psum = ctx.enter_context(tc.psum_pool(name="psum", bufs=8))
 
+        q_rows = keep.tile([P, Q], BF16)
+        nc.vector.memset(q_rows[:].bitcast(I32), 0)
         first = keep.tile([P, 1], F32)
         nc.vector.memset(first[:], 0.0)
-        rows = keep.tile([P, 2, H], BF16)
-        nc.vector.memset(rows[:].rearrange("p a f -> p (a f)").bitcast(I32), 0)
-        ones = keep.tile([P, P], BF16)
+        bias_row = keep.tile([P, H], BF16)
+        nc.vector.memset(bias_row[:].bitcast(I32), 0)
+        ones = keep.tile([P, H], BF16)
         nc.vector.memset(ones[:], 1.0)
-        grouped_xj = keep.tile([P, P * PACK], BF16, align_bytes=64)
+        grouped_jq = keep.tile([P, 2 * P * PACK], BF16, align_bytes=64)
+        grouped_xj = grouped_jq[:, 0 : P * PACK]
+        grouped_q = grouped_jq[:, P * PACK :]
         nc.vector.memset(grouped_xj[0:HALF, :].bitcast(I32), 0)
         grouped_xi = keep.tile([P, P * COPIES * PACK], BF16, align_bytes=64)
         nc.vector.memset(grouped_xi[HALF:P, :].bitcast(I32), 0)
         identity = keep.tile([P, P], F32)
         make_identity(nc, identity[:])
-        nc.scalar.activation(out=first[:], in_=first[:], func=RELU)
 
         x_twice = keep.tile([P, 2, D], BF16)
         for side in range(2):
             nc.sync.dma_start(out=x_twice[:, side, :], in_=x.rearrange("b n d -> (b n) d"))
-        nc.sync.dma_start(out=rows[0:B, 0, :], in_=q)
         w_raw = []
         for c in range(2):
             raw = keep.tile([P, PACK, H], BF16, name="w_raw%d" % c)
             w_rows = g_w0[c * K_PASS : (c + 1) * K_PASS, :]
             nc.sync.dma_start(out=raw[:], in_=w_rows.rearrange("(p t) f -> p t f", t=PACK))
             w_raw.append(raw)
-        nc.sync.dma_start(out=rows[0:1, 1, :], in_=g_b0.rearrange("(o f) -> o f", o=1))
+            if c == 0:
+                nc.sync.dma_start(out=q_rows[0:B, :], in_=q)
+        nc.sync.dma_start(out=bias_row[0:1, :], in_=g_b0.rearrange("(o f) -> o f", o=1))
+        nc.scalar.activation(out=first[:], in_=first[:], func=RELU)
 
         w_grouped = []
         for c in range(2):
@@ -72,11 +79,13 @@ def tile_relationnetwork_pa_kernel(tc, x, q, g_w0, g_b0, out):
         w_scales = keep.tile([P, 2, H], U8, align_bytes=64)
         cut = VECTOR_COLS // 4
 
-        def regroup_w(c):
+        def regroup_w(c, part):
             dst = w_grouped[c][:].rearrange("p (c i) t -> p c t i", i=4)
             src = w_raw[c][:].rearrange("p t (c i) -> p c t i", i=4)
-            nc.vector.tensor_copy(out=dst[:, :cut], in_=src[:, :cut])
-            nc.scalar.copy(out=dst[:, cut:], in_=src[:, cut:])
+            if part == "scalar":
+                nc.scalar.copy(out=dst[:, cut:], in_=src[:, cut:])
+            else:
+                nc.vector.tensor_copy(out=dst[:, :cut], in_=src[:, :cut])
 
         def quantise_w(c):
             nc.vector.quantize_mx(
@@ -97,13 +106,16 @@ def tile_relationnetwork_pa_kernel(tc, x, q, g_w0, g_b0, out):
             )
 
         x_words = x_twice[:].rearrange("p c d -> p (c d)").bitcast(F32)
-        x_t = []
+        x_banks = []
         for reader in range(2):
             x_ps = psum.tile([P, 2, P], F32, name="x_ps", tag="bank")
             for u in range(2):
                 nc.tensor.transpose(x_ps[:, u, :], x_words[:, u : 2 * P : 2], identity[:])
-            x_t.append(x_ps)
-        q_words = rows[:, 0, :].bitcast(F32)
+            x_banks.append(x_ps)
+        idle_ps = psum.tile([P, H], F32, tag="bank")
+        for k in range(WARM[0]):
+            nc.tensor.matmul(out=idle_ps[:], lhsT=ones[:, 0:P], rhs=ones[:], start=True, stop=True)
+        q_words = q_rows[:].bitcast(F32)
         q_ps = psum.tile([P, 2, P], F32, tag="bank")
         for u in range(2):
             nc.tensor.transpose(q_ps[:, u, :], q_words[:, u : 2 * P : 2], identity[:])
@@ -111,27 +123,32 @@ def tile_relationnetwork_pa_kernel(tc, x, q, g_w0, g_b0, out):
         xi_words = grouped_xi[0:HALF, :].bitcast(F32).rearrange(
             "p (m r u) -> p m r u", r=COPIES, u=2
         )
-        for reader, copy in enumerate((nc.scalar.copy, nc.vector.tensor_copy)):
+
+        def copy_facts(copy, reader):
             facts = slice(reader * HALF, (reader + 1) * HALF)
             copy(
                 out=xi_words[:, facts],
-                in_=x_t[reader][0:HALF, :, facts]
+                in_=x_banks[reader][0:HALF, :, facts]
                 .rearrange("p u m -> p m u")
                 .unsqueeze(2)
                 .to_broadcast([HALF, HALF, COPIES, 2]),
             )
-        grouped_q = keep.tile([P, P * PACK], BF16, align_bytes=64)
+
+        copy_facts(nc.scalar.copy, 0)
+        regroup_w(0, "scalar")
         nc.scalar.copy(
-            out=grouped_q[:].bitcast(F32).rearrange("p (b j u) -> p b j u", b=B, u=2),
+            out=grouped_xj[HALF:P, :].bitcast(F32).rearrange("p (m u) -> p m u", u=2),
+            in_=x_banks[0][HALF:P].rearrange("p u m -> p m u"),
+        )
+
+        nc.scalar.copy(
+            out=grouped_q.bitcast(F32).rearrange("p (b j u) -> p b j u", b=B, u=2),
             in_=q_ps[:, :, 0:B]
             .rearrange("p u b -> p b u")
             .unsqueeze(2)
             .to_broadcast([P, B, N, 2]),
         )
-        nc.scalar.copy(
-            out=grouped_xj[HALF:P, :].bitcast(F32).rearrange("p (m u) -> p m u", u=2),
-            in_=x_t[0][HALF:P].rearrange("p u m -> p m u"),
-        )
+        regroup_w(1, "scalar")
 
         def quantise(grouped, name):
             columns = grouped.shape[1] // PACK
@@ -142,22 +159,28 @@ def tile_relationnetwork_pa_kernel(tc, x, q, g_w0, g_b0, out):
             )
             return codes, scales
 
+        regroup_w(0, "vector")
+        copy_facts(nc.vector.tensor_copy, 1)
         xi_codes, xi_scales = quantise(grouped_xi, "xi")
+        regroup_w(1, "vector")
 
-        step_scales = keep.tile([P, N, P], U8, align_bytes=64)
-        step_scale_words = step_scales[:].rearrange("p i m -> p (i m)").bitcast(I32).rearrange(
-            "p (i b w) -> p i b w", i=N, b=B
-        )
         fact_scale_words = xi_scales[:].bitcast(I32).rearrange("p (b i) -> p i b", b=B)
         fact_codes = xi_codes[:].bitcast(I32).rearrange("p (b i r) -> p i b r", b=B, r=COPIES)
+        splits = (0, EARLY_BATCHES * BATCH, N)
+        step_scales = []
 
-        def spread_scales(i0, i1):
+        def spread_scales(part):
+            i0, i1 = splits[part], splits[part + 1]
+            scales = keep.tile([P, i1 - i0, P], U8, name="step_scales%d" % part, align_bytes=64)
             nc.vector.tensor_copy(
-                out=step_scale_words[:, i0:i1],
+                out=scales[:].rearrange("p i m -> p (i m)").bitcast(I32).rearrange(
+                    "p (i b w) -> p i b w", i=i1 - i0, b=B
+                ),
                 in_=fact_scale_words[:, i0:i1]
                 .unsqueeze(3)
                 .to_broadcast([P, i1 - i0, B, N // COPIES]),
             )
+            step_scales.append(scales)
 
         batches = {}
 
@@ -175,40 +198,60 @@ def tile_relationnetwork_pa_kernel(tc, x, q, g_w0, g_b0, out):
             batches[batch] = codes
 
         spread_codes(0, nc.vector.tensor_copy, BATCH)
-        spread_scales(0, EARLY_BATCHES * BATCH)
-        q_codes, q_scales = quantise(grouped_q, "q")
-        xj_codes, xj_scales = quantise(grouped_xj, "xj")
-
-        regroup_w(0)
+        spread_scales(0)
         quantise_w(0)
-        regroup_w(1)
+        jq_codes, jq_scales = quantise(grouped_jq, "jq")
         quantise_w(1)
 
         bias_ps = psum.tile([P, H], F32, tag="bank")
-        nc.tensor.matmul(out=bias_ps[:], lhsT=ones[:], rhs=rows[:, 1, :], start=True, stop=True)
+        nc.tensor.matmul(out=bias_ps[:], lhsT=ones[:, 0:P], rhs=bias_row[:], start=True, stop=True)
+        for k in range(WARM[1]):
+            nc.tensor.matmul(out=idle_ps[:], lhsT=ones[:, 0:P], rhs=ones[:], start=True, stop=True)
         bias_all = keep.tile([P, H], F32)
         nc.scalar.copy(out=bias_all[:], in_=bias_ps[:])
+
+        def fact_i(bank, i, stop):
+            batch, k = divmod(i, BATCH)
+            codes = batches[batch][:, k * P : (k + 1) * P]
+            part = i // splits[1] > 0
+            scales = step_scales[part][:, i - splits[part], :]
+            product(bank, codes, scales, 0, True, stop)
+
+        def fact_j(bank, start):
+            product(bank, jq_codes[:, 0:P], jq_scales[:, 0:P], 0, start, False)
+
+        def question(bank):
+            product(bank, jq_codes[:, P:], jq_scales[:, P:], 1, False, True)
+
+        first_ps = psum.tile([P, H], F32, tag="bank")
+        fact_i(first_ps, 0, False)
+        fact_j(first_ps, False)
+        question(first_ps)
         steady_ps = psum.tile([P, H], F32, tag="bank")
-        product(steady_ps, xj_codes[:], xj_scales[:], 0, True, False)
-        product(steady_ps, q_codes[:], q_scales[:], 1, False, True)
+        fact_j(steady_ps, True)
+        question(steady_ps)
         steady = keep.tile([P, H], F32)
-        nc.vector.tensor_tensor(out=steady[:], in0=steady_ps[:], in1=bias_all[:], op=ADD)
-        spread_codes(1, nc.vector.tensor_copy, BATCH)
 
         out_rows = out.rearrange("b (j i) f -> (b j) i f", i=N)
         for i0 in range(0, N, RUN):
             result = results.tile([P, RUN, H], F32)
-            apart = i0 == 0 or i0 == N - RUN
+            apart = i0 < EDGE or i0 >= N - EDGE
             for s in range(RUN):
                 i = i0 + s
-                batch, k = divmod(i, BATCH)
-                bank = psum.tile([P, H], F32, name="step_ps", tag="bank")
-                product(
-                    bank, batches[batch][:, k * P : (k + 1) * P], step_scales[:, i, :], 0, True, True
-                )
-                nc.vector.tensor_tensor(
-                    out=result[:, s, :], in0=bank[:], in1=steady[:], op=ADD
-                )
+                if i == 0:
+                    nc.vector.tensor_tensor(
+                        out=result[:, s, :], in0=first_ps[:], in1=bias_all[:], op=ADD
+                    )
+                    nc.vector.tensor_tensor(
+                        out=steady[:], in0=steady_ps[:], in1=bias_all[:], op=ADD
+                    )
+                    spread_codes(1, nc.vector.tensor_copy, BATCH)
+                else:
+                    bank = psum.tile([P, H], F32, name="step_ps", tag="bank")
+                    fact_i(bank, i, True)
+                    nc.vector.tensor_tensor(
+                        out=result[:, s, :], in0=bank[:], in1=steady[:], op=ADD
+                    )
                 if apart:
                     if i < N - 1:
                         nc.scalar.activation(out=result[:, s, :], in_=result[:, s, :], func=RELU)
@@ -217,10 +260,10 @@ def tile_relationnetwork_pa_kernel(tc, x, q, g_w0, g_b0, out):
                             out=result[:, s, :], in0=result[:, s, :], scalar1=0.0
                         )
                     nc.sync.dma_start(out=out_rows[:, i, :], in_=result[:, s, :])
-                if i == 1:
-                    spread_scales(EARLY_BATCHES * BATCH, N)
-                if k == BATCH - 1 and batch + EARLY_BATCHES < N // BATCH:
-                    spread_codes(batch + EARLY_BATCHES, nc.gpsimd.tensor_copy, 2)
+                if i == 3:
+                    spread_scales(1)
+                if i % BATCH == BATCH - 1 and i // BATCH + EARLY_BATCHES < N // BATCH:
+                    spread_codes(i // BATCH + EARLY_BATCHES, nc.gpsimd.tensor_copy, 2)
             if not apart:
                 nc.scalar.activation(out=result[:], in_=result[:], func=RELU)
                 nc.sync.dma_start(out=out_rows[:, i0 : i0 + RUN, :], in_=result[:])

@@ -23,9 +23,10 @@ BATCH = 4
 RUN = 2
 EARLY_BATCHES = 2
 WARM = (3, 2)
+WHOLE = 3
 EDGE = 4
 
-VECTOR_COLS = 208
+VECTOR_COLS = 256
 
 FLOPS = 2 * B * N * N * (2 * D + Q) * H
 
@@ -134,11 +135,12 @@ def tile_relationnetwork_pa_kernel(tc, x, q, g_w0, g_b0, out):
                 .to_broadcast([HALF, HALF, COPIES, 2]),
             )
 
-        copy_facts(nc.scalar.copy, 0)
+        copy_facts(nc.vector.tensor_copy, 0)
+        copy_facts(nc.scalar.copy, 1)
         regroup_w(0, "scalar")
         nc.scalar.copy(
             out=grouped_xj[HALF:P, :].bitcast(F32).rearrange("p (m u) -> p m u", u=2),
-            in_=x_banks[0][HALF:P].rearrange("p u m -> p m u"),
+            in_=x_banks[1][HALF:P].rearrange("p u m -> p m u"),
         )
 
         nc.scalar.copy(
@@ -160,7 +162,6 @@ def tile_relationnetwork_pa_kernel(tc, x, q, g_w0, g_b0, out):
             return codes, scales
 
         regroup_w(0, "vector")
-        copy_facts(nc.vector.tensor_copy, 1)
         xi_codes, xi_scales = quantise(grouped_xi, "xi")
         regroup_w(1, "vector")
 
@@ -223,14 +224,21 @@ def tile_relationnetwork_pa_kernel(tc, x, q, g_w0, g_b0, out):
         def question(bank):
             product(bank, jq_codes[:, P:], jq_scales[:, P:], 1, False, True)
 
-        first_ps = psum.tile([P, H], F32, tag="bank")
-        fact_i(first_ps, 0, False)
-        fact_j(first_ps, False)
-        question(first_ps)
-        steady_ps = psum.tile([P, H], F32, tag="bank")
-        fact_j(steady_ps, True)
-        question(steady_ps)
+        whole_banks = []
+        steady_ps = None
+        for i in range(WHOLE):
+            bank = psum.tile([P, H], F32, name="whole_ps", tag="bank")
+            fact_i(bank, i, False)
+            fact_j(bank, False)
+            question(bank)
+            whole_banks.append(bank)
+            if i == WHOLE - 2:
+                steady_ps = psum.tile([P, H], F32, tag="bank")
+                fact_j(steady_ps, True)
+                question(steady_ps)
         steady = keep.tile([P, H], F32)
+        spread_codes(1, nc.vector.tensor_copy, BATCH)
+        spread_scales(1)
 
         out_rows = out.rearrange("b (j i) f -> (b j) i f", i=N)
         for i0 in range(0, N, RUN):
@@ -238,30 +246,28 @@ def tile_relationnetwork_pa_kernel(tc, x, q, g_w0, g_b0, out):
             apart = i0 < EDGE or i0 >= N - EDGE
             for s in range(RUN):
                 i = i0 + s
-                if i == 0:
+                if i < WHOLE:
+                    bank, other = whole_banks[i], bias_all
+                else:
+                    bank, other = psum.tile([P, H], F32, name="step_ps", tag="bank"), steady
+                    fact_i(bank, i, True)
+                pieces = 2 if i == 0 else 1
+                for piece in range(pieces):
+                    cols = slice(piece * H // pieces, (piece + 1) * H // pieces)
+                    value = result[:, s, cols]
                     nc.vector.tensor_tensor(
-                        out=result[:, s, :], in0=first_ps[:], in1=bias_all[:], op=ADD
+                        out=value, in0=bank[:, cols], in1=other[:, cols], op=ADD
                     )
+                    if apart:
+                        if i < N - 1:
+                            nc.scalar.activation(out=value, in_=value, func=RELU)
+                        else:
+                            nc.vector.tensor_scalar_max(out=value, in0=value, scalar1=0.0)
+                        nc.sync.dma_start(out=out_rows[:, i, cols], in_=value)
+                if i == WHOLE - 2:
                     nc.vector.tensor_tensor(
                         out=steady[:], in0=steady_ps[:], in1=bias_all[:], op=ADD
                     )
-                    spread_codes(1, nc.vector.tensor_copy, BATCH)
-                else:
-                    bank = psum.tile([P, H], F32, name="step_ps", tag="bank")
-                    fact_i(bank, i, True)
-                    nc.vector.tensor_tensor(
-                        out=result[:, s, :], in0=bank[:], in1=steady[:], op=ADD
-                    )
-                if apart:
-                    if i < N - 1:
-                        nc.scalar.activation(out=result[:, s, :], in_=result[:, s, :], func=RELU)
-                    else:
-                        nc.vector.tensor_scalar_max(
-                            out=result[:, s, :], in0=result[:, s, :], scalar1=0.0
-                        )
-                    nc.sync.dma_start(out=out_rows[:, i, :], in_=result[:, s, :])
-                if i == 3:
-                    spread_scales(1)
                 if i % BATCH == BATCH - 1 and i // BATCH + EARLY_BATCHES < N // BATCH:
                     spread_codes(i // BATCH + EARLY_BATCHES, nc.gpsimd.tensor_copy, 2)
             if not apart:

@@ -167,13 +167,13 @@ def tile_relationnetwork_pa_kernel(tc, x, q, g_w0, g_b0, out):
 
         fact_scale_words = xi_scales[:].bitcast(I32).rearrange("p (b i) -> p i b", b=B)
         fact_codes = xi_codes[:].bitcast(I32).rearrange("p (b i r) -> p i b r", b=B, r=COPIES)
-        splits = (0, EARLY_BATCHES * BATCH, N)
-        step_scales = []
+        step_scales = {}
 
-        def spread_scales(part):
-            i0, i1 = splits[part], splits[part + 1]
-            scales = keep.tile([P, i1 - i0, P], U8, name="step_scales%d" % part, align_bytes=64)
-            nc.vector.tensor_copy(
+        def spread_scales(batch, count, copy):
+            i0, i1 = batch * BATCH, (batch + count) * BATCH
+            name = "step_scales_of_%d" % count
+            scales = operands.tile([P, i1 - i0, P], U8, name=name, tag=name, align_bytes=64)
+            copy(
                 out=scales[:].rearrange("p i m -> p (i m)").bitcast(I32).rearrange(
                     "p (i b w) -> p i b w", i=i1 - i0, b=B
                 ),
@@ -181,7 +181,8 @@ def tile_relationnetwork_pa_kernel(tc, x, q, g_w0, g_b0, out):
                 .unsqueeze(3)
                 .to_broadcast([P, i1 - i0, B, N // COPIES]),
             )
-            step_scales.append(scales)
+            for i in range(i0, i1):
+                step_scales[i] = scales[:, i - i0, :]
 
         batches = {}
 
@@ -199,7 +200,7 @@ def tile_relationnetwork_pa_kernel(tc, x, q, g_w0, g_b0, out):
             batches[batch] = codes
 
         spread_codes(0, nc.vector.tensor_copy, BATCH)
-        spread_scales(0)
+        spread_scales(0, EARLY_BATCHES, nc.vector.tensor_copy)
         quantise_w(0)
         jq_codes, jq_scales = quantise(grouped_jq, "jq")
         quantise_w(1)
@@ -214,9 +215,7 @@ def tile_relationnetwork_pa_kernel(tc, x, q, g_w0, g_b0, out):
         def fact_i(bank, i, stop):
             batch, k = divmod(i, BATCH)
             codes = batches[batch][:, k * P : (k + 1) * P]
-            part = i // splits[1] > 0
-            scales = step_scales[part][:, i - splits[part], :]
-            product(bank, codes, scales, 0, True, stop)
+            product(bank, codes, step_scales[i], 0, True, stop)
 
         def fact_j(bank, start):
             product(bank, jq_codes[:, 0:P], jq_scales[:, 0:P], 0, start, False)
@@ -238,7 +237,6 @@ def tile_relationnetwork_pa_kernel(tc, x, q, g_w0, g_b0, out):
                 question(steady_ps)
         steady = keep.tile([P, H], F32)
         spread_codes(1, nc.vector.tensor_copy, BATCH)
-        spread_scales(1)
 
         out_rows = out.rearrange("b (j i) f -> (b j) i f", i=N)
         for i0 in range(0, N, RUN):
@@ -269,7 +267,9 @@ def tile_relationnetwork_pa_kernel(tc, x, q, g_w0, g_b0, out):
                         out=steady[:], in0=steady_ps[:], in1=bias_all[:], op=ADD
                     )
                 if i % BATCH == BATCH - 1 and i // BATCH + EARLY_BATCHES < N // BATCH:
-                    spread_codes(i // BATCH + EARLY_BATCHES, nc.gpsimd.tensor_copy, 2)
+                    later = i // BATCH + EARLY_BATCHES
+                    spread_scales(later, 1, nc.gpsimd.tensor_copy)
+                    spread_codes(later, nc.gpsimd.tensor_copy, 2)
             if not apart:
                 nc.scalar.activation(out=result[:], in_=result[:], func=RELU)
                 nc.sync.dma_start(out=out_rows[:, i0 : i0 + RUN, :], in_=result[:])

@@ -20,11 +20,10 @@ K_PASS = P * PACK
 B, N, D, Q, H = 4, 32, 256, 512, 512
 COPIES = 4
 BATCH = 4
-RUN = 2
 EARLY_BATCHES = 2
 WARM = (3, 2)
-WHOLE = 3
-EDGE = 4
+AHEAD = 3
+STORES = (1,) * 8 + (2,) * 11 + (1, 1)
 
 VECTOR_COLS = 256
 
@@ -212,64 +211,50 @@ def tile_relationnetwork_pa_kernel(tc, x, q, g_w0, g_b0, out):
         bias_all = keep.tile([P, H], F32)
         nc.scalar.copy(out=bias_all[:], in_=bias_ps[:])
 
-        def fact_i(bank, i, stop):
+        shared_ps = psum.tile([P, H], F32, tag="bank")
+        product(shared_ps, jq_codes[:, 0:P], jq_scales[:, 0:P], 0, True, True)
+        shared = keep.tile([P, H], F32)
+        nc.vector.tensor_tensor(out=shared[:], in0=shared_ps[:], in1=bias_all[:], op=ADD)
+        spread_codes(1, nc.vector.tensor_copy, BATCH)
+
+        def fact_i(i):
+            bank = psum.tile([P, H], F32, name="step_ps", tag="bank")
             batch, k = divmod(i, BATCH)
             codes = batches[batch][:, k * P : (k + 1) * P]
-            product(bank, codes, step_scales[i], 0, True, stop)
-
-        def fact_j(bank, start):
-            product(bank, jq_codes[:, 0:P], jq_scales[:, 0:P], 0, start, False)
+            product(bank, codes, step_scales[i], 0, True, False)
+            return bank
 
         def question(bank):
             product(bank, jq_codes[:, P:], jq_scales[:, P:], 1, False, True)
 
-        whole_banks = []
-        steady_ps = None
-        for i in range(WHOLE):
-            bank = psum.tile([P, H], F32, name="whole_ps", tag="bank")
-            fact_i(bank, i, False)
-            fact_j(bank, False)
-            question(bank)
-            whole_banks.append(bank)
-            if i == WHOLE - 2:
-                steady_ps = psum.tile([P, H], F32, tag="bank")
-                fact_j(steady_ps, True)
-                question(steady_ps)
-        steady = keep.tile([P, H], F32)
-        spread_codes(1, nc.vector.tensor_copy, BATCH)
-
         out_rows = out.rearrange("b (j i) f -> (b j) i f", i=N)
-        for i0 in range(0, N, RUN):
-            result = results.tile([P, RUN, H], F32)
-            apart = i0 < EDGE or i0 >= N - EDGE
-            for s in range(RUN):
-                i = i0 + s
-                if i < WHOLE:
-                    bank, other = whole_banks[i], bias_all
-                else:
-                    bank, other = psum.tile([P, H], F32, name="step_ps", tag="bank"), steady
-                    fact_i(bank, i, True)
+        banks = [fact_i(i) for i in range(AHEAD)]
+        i = 0
+        for run in STORES:
+            result = results.tile([P, run, H], F32, name="result%d" % run, tag="result%d" % run)
+            for s in range(run):
+                bank = banks[i] if i < AHEAD else fact_i(i)
+                question(bank)
                 pieces = 2 if i == 0 else 1
                 for piece in range(pieces):
                     cols = slice(piece * H // pieces, (piece + 1) * H // pieces)
                     value = result[:, s, cols]
                     nc.vector.tensor_tensor(
-                        out=value, in0=bank[:, cols], in1=other[:, cols], op=ADD
+                        out=value, in0=bank[:, cols], in1=shared[:, cols], op=ADD
                     )
-                    if apart:
+                    if run == 1:
                         if i < N - 1:
                             nc.scalar.activation(out=value, in_=value, func=RELU)
                         else:
                             nc.vector.tensor_scalar_max(out=value, in0=value, scalar1=0.0)
                         nc.sync.dma_start(out=out_rows[:, i, cols], in_=value)
-                if i == WHOLE - 2:
-                    nc.vector.tensor_tensor(
-                        out=steady[:], in0=steady_ps[:], in1=bias_all[:], op=ADD
-                    )
                 if i % BATCH == BATCH - 1 and i // BATCH + EARLY_BATCHES < N // BATCH:
                     later = i // BATCH + EARLY_BATCHES
                     spread_scales(later, 1, nc.gpsimd.tensor_copy)
                     spread_codes(later, nc.gpsimd.tensor_copy, 2)
-            if not apart:
-                nc.scalar.activation(out=result[:], in_=result[:], func=RELU)
-                nc.sync.dma_start(out=out_rows[:, i0 : i0 + RUN, :], in_=result[:])
+                if run > 1 and s % 2 == 1:
+                    pair = result[:, s - 1 : s + 1, :]
+                    nc.scalar.activation(out=pair, in_=pair, func=RELU)
+                i += 1
+            if run > 1:
+                nc.sync.dma_start(out=out_rows[:, i - run : i, :], in_=result[:])

@@ -22,6 +22,7 @@ COPIES = 4
 BATCH = 4
 EARLY_BATCHES = 2
 WARM = (3, 2)
+SUMMED_FROM = 8
 AHEAD = 3
 STORES = (1,) * 8 + (2,) * 11 + (1, 1)
 
@@ -217,30 +218,42 @@ def tile_relationnetwork_pa_kernel(tc, x, q, g_w0, g_b0, out):
         nc.vector.tensor_tensor(out=shared[:], in0=shared_ps[:], in1=bias_all[:], op=ADD)
         spread_codes(1, nc.vector.tensor_copy, BATCH)
 
-        def fact_i(i):
+        def fact_i(i, stop):
             bank = psum.tile([P, H], F32, name="step_ps", tag="bank")
             batch, k = divmod(i, BATCH)
             codes = batches[batch][:, k * P : (k + 1) * P]
-            product(bank, codes, step_scales[i], 0, True, False)
+            product(bank, codes, step_scales[i], 0, True, stop)
             return bank
 
-        def question(bank):
-            product(bank, jq_codes[:, P:], jq_scales[:, P:], 1, False, True)
+        def question(bank, start):
+            product(bank, jq_codes[:, P:], jq_scales[:, P:], 1, start, True)
 
         out_rows = out.rearrange("b (j i) f -> (b j) i f", i=N)
-        banks = [fact_i(i) for i in range(AHEAD)]
+        banks = [fact_i(i, False) for i in range(AHEAD)]
+        waiting = None
         i = 0
         for run in STORES:
             result = results.tile([P, run, H], F32, name="result%d" % run, tag="result%d" % run)
             for s in range(run):
-                bank = banks[i] if i < AHEAD else fact_i(i)
-                question(bank)
+                other = shared if i < SUMMED_FROM else all_shared
+                bank = banks[i] if i < AHEAD else fact_i(i, i >= SUMMED_FROM)
+                if i < SUMMED_FROM:
+                    question(bank, False)
+                if i == 0:
+                    question_ps = psum.tile([P, H], F32, tag="bank")
+                    question(question_ps, True)
+                    question_part = keep.tile([P, H], F32)
+                    nc.scalar.copy(out=question_part[:], in_=question_ps[:])
+                    all_shared = keep.tile([P, H], F32)
+                    nc.gpsimd.tensor_tensor(
+                        out=all_shared[:], in0=question_part[:], in1=shared[:], op=ADD
+                    )
                 pieces = 2 if i == 0 else 1
                 for piece in range(pieces):
                     cols = slice(piece * H // pieces, (piece + 1) * H // pieces)
                     value = result[:, s, cols]
                     nc.vector.tensor_tensor(
-                        out=value, in0=bank[:, cols], in1=shared[:, cols], op=ADD
+                        out=value, in0=bank[:, cols], in1=other[:, cols], op=ADD
                     )
                     if run == 1:
                         if i < N - 1:
@@ -257,4 +270,11 @@ def tile_relationnetwork_pa_kernel(tc, x, q, g_w0, g_b0, out):
                     nc.scalar.activation(out=pair, in_=pair, func=RELU)
                 i += 1
             if run > 1:
-                nc.sync.dma_start(out=out_rows[:, i - run : i, :], in_=result[:])
+                if waiting is not None:
+                    nc.scalar.dma_start(out=waiting[0], in_=waiting[1])
+                    waiting = None
+                rows = out_rows[:, i - run : i, :]
+                if i // run % 2 and i < N - 2 * run:
+                    waiting = (rows, result[:])
+                else:
+                    nc.sync.dma_start(out=rows, in_=result[:])

from contextlib import ExitStack

import concourse.mybir as mybir
from concourse.masks import make_identity

FP8X4 = mybir.dt.float8_e4m3fn_x4
BF16 = mybir.dt.bfloat16
F32 = mybir.dt.float32
I32 = mybir.dt.int32
U32 = mybir.dt.uint32
U8 = mybir.dt.uint8
ADD = mybir.AluOpType.add
RELU = mybir.ActivationFunctionType.Relu

P = 128
HALF = P // 2
PACK = 4
K_PASS = P * PACK

B, N, D, Q, H = 4, 32, 256, 512, 512
COPIES = 4
BATCH = 4
EARLY_BATCHES = 2
WARM = (3, 2)
SUMMED_FROM = 8
AHEAD = 3
STORES = (1,) * 8 + (2,) * 11 + (1, 1)

VECTOR_COLS = 256

FLOPS = 2 * B * N * N * (2 * D + Q) * H


def tile_relationnetwork_pa_kernel(tc, x, q, g_w0, g_b0, out):
    nc = tc.nc
    with ExitStack() as ctx:
        ctx.enter_context(tc.manual_schedule())
        keep = ctx.enter_context(tc.tile_pool(name="keep", bufs=1))
        operands = ctx.enter_context(tc.tile_pool(name="operands", bufs=EARLY_BATCHES))
        results = ctx.enter_context(tc.tile_pool(name="results", bufs=8))
        psum = ctx.enter_context(tc.psum_pool(name="psum", bufs=8))

        q_rows = keep.tile([P, Q], BF16)
        nc.vector.memset(q_rows[:].bitcast(I32), 0)
        first = keep.tile([P, 1], F32)
        nc.vector.memset(first[:], 0.0)
        bias_row = keep.tile([P, H], BF16)
        nc.vector.memset(bias_row[:].bitcast(I32), 0)
        ones = keep.tile([P, H], BF16)
        nc.vector.memset(ones[:], 1.0)
        grouped_jq = keep.tile([P, 2 * P * PACK], BF16, align_bytes=64)
        grouped_xj = grouped_jq[:, 0 : P * PACK]
        grouped_q = grouped_jq[:, P * PACK :]
        nc.vector.memset(grouped_xj[0:HALF, :].bitcast(I32), 0)
        grouped_xi = keep.tile([P, P * COPIES * PACK], BF16, align_bytes=64)
        nc.vector.memset(grouped_xi[HALF:P, :].bitcast(I32), 0)
        identity = keep.tile([P, P], F32)
        make_identity(nc, identity[:])

        x_twice = keep.tile([P, 2, D], BF16)
        for side in range(2):
            nc.sync.dma_start(out=x_twice[:, side, :], in_=x.rearrange("b n d -> (b n) d"))
        w_raw = []
        for c in range(2):
            raw = keep.tile([P, PACK, H], BF16, name="w_raw%d" % c)
            w_rows = g_w0[c * K_PASS : (c + 1) * K_PASS, :]
            nc.sync.dma_start(out=raw[:], in_=w_rows.rearrange("(p t) f -> p t f", t=PACK))
            w_raw.append(raw)
            if c == 0:
                nc.sync.dma_start(out=q_rows[0:B, :], in_=q)
        nc.sync.dma_start(out=bias_row[0:1, :], in_=g_b0.rearrange("(o f) -> o f", o=1))
        nc.scalar.activation(out=first[:], in_=first[:], func=RELU)

        w_grouped = []
        for c in range(2):
            w_grouped.append(
                keep.tile([P, H, PACK], BF16, name="w_grouped%d" % c, align_bytes=64)
            )
        w_codes = keep.tile([P, 2, H], U32, align_bytes=64)
        w_scales = keep.tile([P, 2, H], U8, align_bytes=64)
        cut = VECTOR_COLS // 4

        def regroup_w(c, part):
            dst = w_grouped[c][:].rearrange("p (c i) t -> p c t i", i=4)
            src = w_raw[c][:].rearrange("p t (c i) -> p c t i", i=4)
            if part == "scalar":
                nc.scalar.copy(out=dst[:, cut:], in_=src[:, cut:])
            else:
                nc.vector.tensor_copy(out=dst[:, :cut], in_=src[:, :cut])

        def quantise_w(c):
            nc.vector.quantize_mx(
                out=w_codes[:, c, :].bitcast(FP8X4),
                scales=w_scales[:, c, :],
                in_=w_grouped[c][:].rearrange("p f t -> p (f t)"),
            )

        def product(bank, codes, scales, c, start, stop):
            nc.tensor.matmul_mx(
                out=bank[:],
                lhsT=codes.bitcast(FP8X4),
                lhsT_scale=scales,
                rhs=w_codes[:, c, :].bitcast(FP8X4),
                rhs_scale=w_scales[:, c, :],
                start=start,
                stop=stop,
            )

        x_words = x_twice[:].rearrange("p c d -> p (c d)").bitcast(F32)
        x_banks = []
        for reader in range(2):
            x_ps = psum.tile([P, 2, P], F32, name="x_ps", tag="bank")
            for u in range(2):
                nc.tensor.transpose(x_ps[:, u, :], x_words[:, u : 2 * P : 2], identity[:])
            x_banks.append(x_ps)
        idle_ps = psum.tile([P, H], F32, tag="bank")
        for k in range(WARM[0]):
            nc.tensor.matmul(out=idle_ps[:], lhsT=ones[:, 0:P], rhs=ones[:], start=True, stop=True)
        q_words = q_rows[:].bitcast(F32)
        q_ps = psum.tile([P, 2, P], F32, tag="bank")
        for u in range(2):
            nc.tensor.transpose(q_ps[:, u, :], q_words[:, u : 2 * P : 2], identity[:])

        xi_words = grouped_xi[0:HALF, :].bitcast(F32).rearrange(
            "p (m r u) -> p m r u", r=COPIES, u=2
        )

        def copy_facts(copy, reader):
            facts = slice(reader * HALF, (reader + 1) * HALF)
            copy(
                out=xi_words[:, facts],
                in_=x_banks[reader][0:HALF, :, facts]
                .rearrange("p u m -> p m u")
                .unsqueeze(2)
                .to_broadcast([HALF, HALF, COPIES, 2]),
            )

        copy_facts(nc.vector.tensor_copy, 0)
        copy_facts(nc.scalar.copy, 1)
        regroup_w(0, "scalar")
        nc.scalar.copy(
            out=grouped_xj[HALF:P, :].bitcast(F32).rearrange("p (m u) -> p m u", u=2),
            in_=x_banks[1][HALF:P].rearrange("p u m -> p m u"),
        )

        nc.scalar.copy(
            out=grouped_q.bitcast(F32).rearrange("p (b j u) -> p b j u", b=B, u=2),
            in_=q_ps[:, :, 0:B]
            .rearrange("p u b -> p b u")
            .unsqueeze(2)
            .to_broadcast([P, B, N, 2]),
        )
        regroup_w(1, "scalar")

        def quantise(grouped, name):
            columns = grouped.shape[1] // PACK
            codes = keep.tile([P, columns], U32, name=name + "_codes", align_bytes=64)
            scales = keep.tile([P, columns], U8, name=name + "_scales", align_bytes=64)
            nc.vector.quantize_mx(
                out=codes[:].bitcast(FP8X4), scales=scales[:], in_=grouped[:]
            )
            return codes, scales

        regroup_w(0, "vector")
        xi_codes, xi_scales = quantise(grouped_xi, "xi")
        regroup_w(1, "vector")

        fact_scale_words = xi_scales[:].bitcast(I32).rearrange("p (b i) -> p i b", b=B)
        fact_codes = xi_codes[:].bitcast(I32).rearrange("p (b i r) -> p i b r", b=B, r=COPIES)
        step_scales = {}

        def spread_scales(batch, count, copy):
            i0, i1 = batch * BATCH, (batch + count) * BATCH
            name = "step_scales_of_%d" % count
            scales = operands.tile([P, i1 - i0, P], U8, name=name, tag=name, align_bytes=64)
            copy(
                out=scales[:].rearrange("p i m -> p (i m)").bitcast(I32).rearrange(
                    "p (i b w) -> p i b w", i=i1 - i0, b=B
                ),
                in_=fact_scale_words[:, i0:i1]
                .unsqueeze(3)
                .to_broadcast([P, i1 - i0, B, N // COPIES]),
            )
            for i in range(i0, i1):
                step_scales[i] = scales[:, i - i0, :]

        batches = {}

        def spread_codes(batch, copy, at_once):
            codes = operands.tile([P, BATCH * P], U32, name="step_codes", align_bytes=64)
            words = codes[:].bitcast(I32).rearrange("p (i b j) -> p i b j", i=BATCH, b=B)
            for k in range(0, BATCH, at_once):
                i0 = batch * BATCH + k
                copy(
                    out=words[:, k : k + at_once],
                    in_=fact_codes[:, i0 : i0 + at_once, :, 0]
                    .unsqueeze(3)
                    .to_broadcast([P, at_once, B, N]),
                )
            batches[batch] = codes

        spread_codes(0, nc.vector.tensor_copy, BATCH)
        spread_scales(0, EARLY_BATCHES, nc.vector.tensor_copy)
        quantise_w(0)
        jq_codes, jq_scales = quantise(grouped_jq, "jq")
        quantise_w(1)

        bias_ps = psum.tile([P, H], F32, tag="bank")
        nc.tensor.matmul(out=bias_ps[:], lhsT=ones[:, 0:P], rhs=bias_row[:], start=True, stop=True)
        for k in range(WARM[1]):
            nc.tensor.matmul(out=idle_ps[:], lhsT=ones[:, 0:P], rhs=ones[:], start=True, stop=True)
        bias_all = keep.tile([P, H], F32)
        nc.scalar.copy(out=bias_all[:], in_=bias_ps[:])

        shared_ps = psum.tile([P, H], F32, tag="bank")
        product(shared_ps, jq_codes[:, 0:P], jq_scales[:, 0:P], 0, True, True)
        shared = keep.tile([P, H], F32)
        nc.vector.tensor_tensor(out=shared[:], in0=shared_ps[:], in1=bias_all[:], op=ADD)
        spread_codes(1, nc.vector.tensor_copy, BATCH)

        def fact_i(i, stop):
            bank = psum.tile([P, H], F32, name="step_ps", tag="bank")
            batch, k = divmod(i, BATCH)
            codes = batches[batch][:, k * P : (k + 1) * P]
            product(bank, codes, step_scales[i], 0, True, stop)
            return bank

        def question(bank, start):
            product(bank, jq_codes[:, P:], jq_scales[:, P:], 1, start, True)

        out_rows = out.rearrange("b (j i) f -> (b j) i f", i=N)
        banks = [fact_i(i, False) for i in range(AHEAD)]
        waiting = None
        i = 0
        for run in STORES:
            result = results.tile([P, run, H], F32, name="result%d" % run, tag="result%d" % run)
            for s in range(run):
                other = shared if i < SUMMED_FROM else all_shared
                bank = banks[i] if i < AHEAD else fact_i(i, i >= SUMMED_FROM)
                if i < SUMMED_FROM:
                    question(bank, False)
                if i == 0:
                    question_ps = psum.tile([P, H], F32, tag="bank")
                    question(question_ps, True)
                    question_part = keep.tile([P, H], F32)
                    nc.scalar.copy(out=question_part[:], in_=question_ps[:])
                    all_shared = keep.tile([P, H], F32)
                    nc.gpsimd.tensor_tensor(
                        out=all_shared[:], in0=question_part[:], in1=shared[:], op=ADD
                    )
                pieces = 2 if i == 0 else 1
                for piece in range(pieces):
                    cols = slice(piece * H // pieces, (piece + 1) * H // pieces)
                    value = result[:, s, cols]
                    nc.vector.tensor_tensor(
                        out=value, in0=bank[:, cols], in1=other[:, cols], op=ADD
                    )
                    if run == 1:
                        if i < N - 1:
                            nc.scalar.activation(out=value, in_=value, func=RELU)
                        else:
                            nc.vector.tensor_scalar_max(out=value, in0=value, scalar1=0.0)
                        nc.sync.dma_start(out=out_rows[:, i, cols], in_=value)
                if i % BATCH == BATCH - 1 and i // BATCH + EARLY_BATCHES < N // BATCH:
                    later = i // BATCH + EARLY_BATCHES
                    spread_scales(later, 1, nc.gpsimd.tensor_copy)
                    spread_codes(later, nc.gpsimd.tensor_copy, 2)
                if run > 1 and s % 2 == 1:
                    pair = result[:, s - 1 : s + 1, :]
                    nc.scalar.activation(out=pair, in_=pair, func=RELU)
                i += 1
            if run > 1:
                if waiting is not None:
                    nc.scalar.dma_start(out=waiting[0], in_=waiting[1])
                    waiting = None
                rows = out_rows[:, i - run : i, :]
                if i // run % 2 and i < N - 2 * run:
                    waiting = (rows, result[:])
                else:
                    nc.sync.dma_start(out=rows, in_=result[:])
